import numpy as np
import ml_dtypes


def mxq(x, axis, fmt="e4m3"):
    dtype, down = {"e4m3": (ml_dtypes.float8_e4m3fn, 7), "e5m2": (ml_dtypes.float8_e5m2, 14)}[fmt]
    v = np.moveaxis(np.asarray(x, np.float32).astype(ml_dtypes.bfloat16).astype(np.float64), axis, -1)
    blocks = v.reshape(v.shape[:-1] + (-1, 32))
    amax = np.abs(blocks).max(-1, keepdims=True)
    byte = np.maximum(np.where(amax > 0, np.frexp(amax)[1] - 1 + 127, 0) - down, 1)
    scale = np.exp2(byte - 127.0)
    codes = (blocks / scale).astype(np.float32).astype(dtype).astype(np.float64)
    return np.moveaxis((codes * scale).reshape(v.shape), -1, axis)


WIDE = False


def mx_kscale(k):
    if not WIDE:
        return np.ones(k)
    levels = np.array([10, -10, 5, -5, 0])
    if k % 512:
        return np.exp2(np.random.permutation(np.resize(levels, k // 32))).repeat(32)
    a = np.empty((k // 512, 16))
    for p in range(k // 512):
        a[p, :8] = np.random.permutation(np.resize(levels, 8))
        for g in range(8):
            far = levels[np.abs(levels - a[p, g]) >= 10]
            a[p, g + 8] = far[np.random.randint(len(far))]
    return np.exp2(a.ravel()).repeat(32)


BF16 = ml_dtypes.bfloat16


def bf(x):
    return np.asarray(x, np.float32).astype(BF16)


def f64(x):
    return np.asarray(x).astype(np.float64)


B, D, H, F, K = 2048, 1024, 1024, 1024, 128
EPS_LN = 1e-5


def silu(v):
    return v / (1.0 + np.exp(-v))


def draw0():
    s = mx_kscale(D)
    return {"x": bf(np.random.standard_normal((B, D)) * s),
            "W1": bf(np.random.standard_normal((D, H)) / np.sqrt(D) / s[:, None]),
            "b1": bf(0.2 * np.random.standard_normal(H)),
            "g": bf(1.0 + 0.1 * np.random.standard_normal(H)),
            "beta": bf(0.1 * np.random.standard_normal(H))}


def core(x, W1, b1, g, beta):
    h = silu((mxq(f64(x), 1, "e4m3") @ mxq(f64(W1), 0, "e4m3")) + f64(b1))
    mu = h.mean(-1, keepdims=True)
    var = ((h - mu) ** 2).mean(-1, keepdims=True)
    return (h - mu) / np.sqrt(var + EPS_LN) * f64(g) + f64(beta)


def e4m3fn_bytes(y):
    return np.clip(np.asarray(y, np.float64), -448.0, 448.0).astype(np.float32).astype(ml_dtypes.float8_e4m3fn).view(np.uint8)


def e4m3fn_values(b):
    return np.asarray(b, np.uint8).view(ml_dtypes.float8_e4m3fn).astype(np.float64)


def setup_inputs():
    d = draw0()
    x0 = np.asarray(d['x']).astype(np.float64)
    s = (np.max(np.abs(x0), axis=(0,), keepdims=True) / 448.0).astype(np.float32)
    out = {}
    for k, v in d.items():
        if k == 'x':
            out['x_bytes'] = e4m3fn_bytes(x0 / s.astype(np.float64))
            out['x_scale'] = s
        else:
            out[k] = v
    return out


def reference(x_bytes, x_scale, W1, b1, g, beta):
    return core(e4m3fn_values(x_bytes) * x_scale.astype(np.float64), W1, b1, g, beta)

@@ -1,0 +1,239 @@
+from contextlib import ExitStack
+
+import concourse.mybir as mybir
+from concourse.masks import make_identity
+
+B, D, H = 2048, 1024, 1024
+FLOPS = 2 * B * D * H
+EPS_LN = 1e-5
+
+F32 = mybir.dt.float32
+BF16 = mybir.dt.bfloat16
+U32 = mybir.dt.uint32
+U8 = mybir.dt.uint8
+FP8 = mybir.dt.float8_e4m3fn
+FP8X4 = mybir.dt.float8_e4m3fn_x4
+ACT = mybir.ActivationFunctionType
+ALU = mybir.AluOpType
+
+P = 128
+NT = B // P
+GT = 4
+NG = NT // GT
+NCB = H // P
+NPASS = D // 512
+
+
+def tile_evidentialhead_pa_kernel(tc, x_bytes, x_scale, W1, b1, g, beta, out):
+    nc = tc.nc
+    with ExitStack() as ctx:
+        keep = ctx.enter_context(tc.tile_pool(name="keep", bufs=1))
+        stage = ctx.enter_context(tc.tile_pool(name="stage", bufs=2))
+        small = ctx.enter_context(tc.tile_pool(name="small", bufs=4))
+        ps_hs = ctx.enter_context(tc.psum_pool(name="pshs", bufs=1))
+        ps_be = ctx.enter_context(tc.psum_pool(name="psbe", bufs=1))
+        ps_t = ctx.enter_context(tc.psum_pool(name="pst", bufs=6))
+
+        sc_b = keep.tile([P, D], F32, name="sc_b", tag="sc_b")
+        nc.scalar.dma_start(out=sc_b[:], in_=x_scale.rearrange("o k -> (o k)").partition_broadcast(P))
+        b1c = keep.tile([P, NCB], BF16, name="b1c", tag="b1c")
+        beta_c = keep.tile([P, NCB], BF16, name="beta_c", tag="beta_c")
+        with nc.allow_non_contiguous_dma(reason="bias and shift: one element a partition, 1024 elements each, once"):
+            nc.scalar.dma_start(out=b1c[:], in_=b1.rearrange("(c p) -> p c", p=P))
+            nc.scalar.dma_start(out=beta_c[:], in_=beta.rearrange("(c p) -> p c", p=P))
+
+        w_view = W1.rearrange("(s p j) n -> s p j n", s=NPASS, j=4)
+        x_view = x_bytes.rearrange("(a i p) k -> a p i k", a=NG, i=GT)
+        wraw = {}
+        xby = {}
+
+        def load_w(s, nh):
+            t = keep.tile([P, 4, 512], BF16, name="wraw%d%d" % (s, nh), tag="wraw%d%d" % (s, nh))
+            nc.sync.dma_start(out=t[:], in_=w_view[s, :, :, nh * 512:(nh + 1) * 512])
+            wraw[(s, nh)] = t
+
+        def load_x(a, per_tile):
+            t = keep.tile([P, GT, D], U8, name="xbytes%d" % a, tag="xbytes%d" % a)
+            xby[a] = t
+            if not per_tile:
+                nc.sync.dma_start(out=t[:], in_=x_view[a])
+
+        def load_x_tile(a, il):
+            nc.sync.dma_start(out=xby[a][:, il, :], in_=x_view[a, :, il, :])
+
+        load_x(0, True)
+        load_x_tile(0, 0)
+        load_w(0, 0)
+        load_x_tile(0, 1)
+        load_w(1, 0)
+        load_x_tile(0, 2)
+        load_x_tile(0, 3)
+        load_w(0, 1)
+        load_w(1, 1)
+        load_x(1, False)
+        load_x(2, False)
+        load_x(3, False)
+        g_b = keep.tile([P, H], BF16, name="g_b", tag="g_b")
+        nc.sync.dma_start(out=g_b[:], in_=g.partition_broadcast(P))
+
+        warm = keep.tile([P, 1], F32, name="warm", tag="warm")
+        nc.vector.memset(warm[:], 0.0)
+        warm2 = keep.tile([P, 1], F32, name="warm2", tag="warm2")
+        nc.scalar.activation(out=warm2[:], in_=warm[:], func=ACT.Silu)
+        ident = keep.tile([P, P], F32, name="ident", tag="ident")
+        make_identity(nc, ident[:])
+        ident_bf = keep.tile([P, P], BF16, name="ident_bf", tag="ident_bf")
+        make_identity(nc, ident_bf[:])
+        beta_ps = ps_be.tile([P, H], BF16, name="beta_ps", tag="beta_ps")
+        neghalf = keep.tile([P, 1], F32, name="neghalf", tag="neghalf")
+        nc.vector.memset(neghalf[:], -0.5)
+        b1f = keep.tile([P, NCB], F32, name="b1f", tag="b1f")
+        nc.gpsimd.tensor_copy(out=b1f[:], in_=b1c[:])
+
+        wq = keep.tile([P, NPASS * H], U32, name="wq", tag="wq", align_bytes=64)
+        ws = keep.tile([P, NPASS * H], U8, name="ws", tag="ws", align_bytes=64)
+        xg = {}
+        xq = {}
+        xs = {}
+        for a in range(NG):
+            xg[a] = keep.tile([P, NPASS * 512 * 4], BF16, name="xg%d" % a, tag="xg%d" % a, align_bytes=64)
+            xq[a] = keep.tile([P, NPASS * 512], U32, name="xq%d" % a, tag="xq%d" % a, align_bytes=64)
+            xs[a] = keep.tile([P, NPASS * 512], U8, name="xs%d" % a, tag="xs%d" % a, align_bytes=64)
+        wgs = {}
+        hT = {}
+        ys = {}
+        rstds = {}
+
+        def w_interleave(s, nh, eng):
+            wg = stage.tile([P, 512, 4], BF16, name="wg", tag="wg", align_bytes=64)
+            src = wraw[(s, nh)][:].rearrange("p j n -> p n j")
+            if eng == "v":
+                nc.vector.tensor_copy(out=wg[:], in_=src)
+            else:
+                nc.scalar.copy(out=wg[:], in_=src)
+            wgs[(s, nh)] = wg
+
+        def w_quant(s, nh):
+            c0 = s * H + nh * 512
+            nc.vector.quantize_mx(
+                out=wq[:, c0:c0 + 512].bitcast(FP8X4),
+                scales=ws[:, c0:c0 + 512],
+                in_=wgs[(s, nh)][:].rearrange("p n j -> p (n j)"),
+            )
+
+        def x_prep(i):
+            a, il = divmod(i, GT)
+            xb = stage.tile([P, D], BF16, name="xb", tag="xb", bufs=3)
+            nc.vector.tensor_tensor(out=xb[:], in0=xby[a][:, il, :].bitcast(FP8), in1=sc_b[:], op=ALU.mult)
+            words = xb[:].bitcast(F32)
+            xt_bank = ps_t.tile([P, 512], F32, name="tb", tag="tb")
+            xt = xt_bank[:].rearrange("p (s u r) -> p s u r", s=NPASS, u=2)
+            for s in range(NPASS):
+                for u in range(2):
+                    nc.tensor.transpose(xt[:, s, u, :], words[:, 256 * s + u:256 * (s + 1):2], ident[:])
+            xgw = xg[a][:].bitcast(F32).rearrange("p (s r u) -> p s r u", s=NPASS, u=2)
+            nc.scalar.copy(out=xgw[:, :, il * P:(il + 1) * P, :], in_=xt.rearrange("p s u r -> p s r u"))
+
+        def x_quant(a):
+            nc.vector.quantize_mx(out=xq[a][:].bitcast(FP8X4), scales=xs[a][:], in_=xg[a][:])
+
+        def mm_silu(a, cb):
+            if cb == 0:
+                hT[a] = stage.tile([P, NCB, 512], F32, name="hT", tag="hT", bufs=3)
+            mm = ps_t.tile([P, 512], F32, name="tb", tag="tb")
+            for s in range(NPASS):
+                c0 = s * H + cb * P
+                nc.tensor.matmul_mx(
+                    out=mm[:],
+                    lhsT=wq[:, c0:c0 + P].bitcast(FP8X4),
+                    lhsT_scale=ws[:, c0:c0 + P],
+                    rhs=xq[a][:, s * 512:(s + 1) * 512].bitcast(FP8X4),
+                    rhs_scale=xs[a][:, s * 512:(s + 1) * 512],
+                    start=(s == 0),
+                    stop=(s == NPASS - 1),
+                )
+            nc.scalar.activation(out=hT[a][:, cb, :], in_=mm[:], func=ACT.Silu, bias=b1f[:, cb:cb + 1])
+
+        def epi1(i):
+            a, il = divmod(i, GT)
+            ts = slice(il * P, (il + 1) * P)
+            hs = ps_hs.tile([P, P], F32, name="hs", tag="hs")
+            for cb in range(NCB):
+                nc.tensor.matmul(out=hs[:], lhsT=hT[a][:, cb, ts], rhs=ident[:],
+                                 start=(cb == 0), stop=(cb == NCB - 1), is_transpose=True)
+            negmu = small.tile([P, 1], F32, name="negmu", tag="negmu")
+            junk = stage.tile([P, 512], BF16, name="junk", tag="junk")
+            nc.scalar.activation(out=junk[:, 0:P], in_=hs[:], func=ACT.Identity, scale=-1.0 / H, accum_out=negmu[:])
+            hts = []
+            for half in range(2):
+                ht = ps_t.tile([P, 512], F32, name="tb", tag="tb")
+                for j in range(4):
+                    nc.tensor.transpose(ht[:, j * P:(j + 1) * P], hT[a][:, 4 * half + j, ts], ident[:])
+                hts.append(ht)
+            ssq = small.tile([P, 2], F32, name="ssq", tag="ssq")
+            for half in range(2):
+                junk2 = stage.tile([P, 512], BF16, name="junk", tag="junk")
+                nc.scalar.activation(out=junk2[:], in_=hts[half][:], func=ACT.Square, bias=negmu[:],
+                                     accum_out=ssq[:, half:half + 1])
+            y = stage.tile([P, H], F32, name="y", tag="y", bufs=4)
+            for half in range(2):
+                cs = slice(half * 512, (half + 1) * 512)
+                nc.vector.scalar_tensor_tensor(out=y[:, cs], in0=hts[half][:], scalar=negmu[:], in1=g_b[:, cs],
+                                               op0=ALU.add, op1=ALU.mult)
+            ve = small.tile([P, 1], F32, name="ve", tag="ve")
+            junk3 = small.tile([P, 2], F32, name="junk3", tag="junk3")
+            nc.scalar.activation(out=junk3[:], in_=ssq[:], func=ACT.Copy, scale=1.0 / H, bias=EPS_LN / 2.0,
+                                 accum_out=ve[:])
+            rstd = small.tile([P, 1], F32, name="rstd", tag="rstd")
+            nc.gpsimd.tensor_tensor(out=rstd[:], in0=ve[:], in1=neghalf[:], op=ALU.pow)
+            ys[i] = y
+            rstds[i] = rstd
+
+        def epi2(i):
+            o = stage.tile([P, H], F32, name="o", tag="o", bufs=3)
+            pieces = 2 if i == NT - 1 else 1
+            w = H // pieces
+            for c in range(pieces):
+                cs = slice(c * w, (c + 1) * w)
+                nc.vector.scalar_tensor_tensor(out=o[:, cs], in0=ys[i][:, cs], scalar=rstds[i][:], in1=beta_ps[:, cs],
+                                               op0=ALU.mult, op1=ALU.add)
+                nc.sync.dma_start(out=out[i * P:(i + 1) * P, cs], in_=o[:, cs])
+
+        xper = [1, 2, 2, 2, 1, 1, 1, 1, 1]
+        LAG = 5
+        w_interleave(1, 0, "v")
+        x_prep(0)
+        w_interleave(0, 0, "s")
+        w_quant(1, 0)
+        x_prep(1)
+        w_interleave(1, 1, "s")
+        x_prep(2)
+        x_prep(3)
+        w_quant(0, 0)
+        x_quant(0)
+
+        nx = GT
+        for t in range(NT + LAG + 1):
+            if LAG <= t < NT + LAG:
+                epi1(t - LAG)
+            if t < NT:
+                a, q = divmod(t, GT)
+                mm_silu(a, 2 * q)
+                mm_silu(a, 2 * q + 1)
+                if t == 0:
+                    w_interleave(0, 1, "s")
+                    w_quant(1, 1)
+                if t == 1:
+                    w_quant(0, 1)
+                    for cb in range(NCB):
+                        nc.tensor.matmul(out=beta_ps[:, cb * P:(cb + 1) * P],
+                                         lhsT=beta_c[:, cb:cb + 1].to_broadcast([P, P]), rhs=ident_bf[:],
+                                         start=True, stop=True)
+            for rep in range(xper[t] if t < len(xper) else 0):
+                if nx < NT:
+                    x_prep(nx)
+                    if nx % GT == GT - 1:
+                        x_quant(nx // GT)
+                    nx += 1
+            if t >= LAG + 1:
+                epi2(t - LAG - 1)

@@ -31,16 +31,13 @@ def tile_evidentialhead_pa_kernel(tc, x_bytes, x_scale, W1, b1, g, beta, out):
         stage = ctx.enter_context(tc.tile_pool(name="stage", bufs=2))
         small = ctx.enter_context(tc.tile_pool(name="small", bufs=4))
         ps_hs = ctx.enter_context(tc.psum_pool(name="pshs", bufs=1))
-        ps_be = ctx.enter_context(tc.psum_pool(name="psbe", bufs=1))
-        ps_t = ctx.enter_context(tc.psum_pool(name="pst", bufs=6))
+        ps_t = ctx.enter_context(tc.psum_pool(name="pst", bufs=7))
 
         sc_b = keep.tile([P, D], F32, name="sc_b", tag="sc_b")
         nc.scalar.dma_start(out=sc_b[:], in_=x_scale.rearrange("o k -> (o k)").partition_broadcast(P))
         b1c = keep.tile([P, NCB], BF16, name="b1c", tag="b1c")
-        beta_c = keep.tile([P, NCB], BF16, name="beta_c", tag="beta_c")
-        with nc.allow_non_contiguous_dma(reason="bias and shift: one element a partition, 1024 elements each, once"):
+        with nc.allow_non_contiguous_dma(reason="bias: one element a partition, 1024 elements, once"):
             nc.scalar.dma_start(out=b1c[:], in_=b1.rearrange("(c p) -> p c", p=P))
-            nc.scalar.dma_start(out=beta_c[:], in_=beta.rearrange("(c p) -> p c", p=P))
 
         w_view = W1.rearrange("(s p j) n -> s p j n", s=NPASS, j=4)
         x_view = x_bytes.rearrange("(a i p) k -> a p i k", a=NG, i=GT)
@@ -75,6 +72,8 @@ def tile_evidentialhead_pa_kernel(tc, x_bytes, x_scale, W1, b1, g, beta, out):
         load_x(3, False)
         g_b = keep.tile([P, H], BF16, name="g_b", tag="g_b")
         nc.sync.dma_start(out=g_b[:], in_=g.partition_broadcast(P))
+        beta_b = keep.tile([P, H], BF16, name="beta_b", tag="beta_b")
+        nc.sync.dma_start(out=beta_b[:], in_=beta.partition_broadcast(P))
 
         warm = keep.tile([P, 1], F32, name="warm", tag="warm")
         nc.vector.memset(warm[:], 0.0)
@@ -82,9 +81,6 @@ def tile_evidentialhead_pa_kernel(tc, x_bytes, x_scale, W1, b1, g, beta, out):
         nc.scalar.activation(out=warm2[:], in_=warm[:], func=ACT.Silu)
         ident = keep.tile([P, P], F32, name="ident", tag="ident")
         make_identity(nc, ident[:])
-        ident_bf = keep.tile([P, P], BF16, name="ident_bf", tag="ident_bf")
-        make_identity(nc, ident_bf[:])
-        beta_ps = ps_be.tile([P, H], BF16, name="beta_ps", tag="beta_ps")
         neghalf = keep.tile([P, 1], F32, name="neghalf", tag="neghalf")
         nc.vector.memset(neghalf[:], -0.5)
         b1f = keep.tile([P, NCB], F32, name="b1f", tag="b1f")
@@ -195,7 +191,7 @@ def tile_evidentialhead_pa_kernel(tc, x_bytes, x_scale, W1, b1, g, beta, out):
             w = H // pieces
             for c in range(pieces):
                 cs = slice(c * w, (c + 1) * w)
-                nc.vector.scalar_tensor_tensor(out=o[:, cs], in0=ys[i][:, cs], scalar=rstds[i][:], in1=beta_ps[:, cs],
+                nc.vector.scalar_tensor_tensor(out=o[:, cs], in0=ys[i][:, cs], scalar=rstds[i][:], in1=beta_b[:, cs],
                                                op0=ALU.mult, op1=ALU.add)
                 nc.sync.dma_start(out=out[i * P:(i + 1) * P, cs], in_=o[:, cs])
 
@@ -225,10 +221,6 @@ def tile_evidentialhead_pa_kernel(tc, x_bytes, x_scale, W1, b1, g, beta, out):
                     w_quant(1, 1)
                 if t == 1:
                     w_quant(0, 1)
-                    for cb in range(NCB):
-                        nc.tensor.matmul(out=beta_ps[:, cb * P:(cb + 1) * P],
-                                         lhsT=beta_c[:, cb:cb + 1].to_broadcast([P, P]), rhs=ident_bf[:],
-                                         start=True, stop=True)
             for rep in range(xper[t] if t < len(xper) else 0):
                 if nx < NT:
                     x_prep(nx)

@@ -59,10 +59,10 @@ def tile_evidentialhead_pa_kernel(tc, x_bytes, x_scale, W1, b1, g, beta, out):
             nc.sync.dma_start(out=xby[a][:, il, :], in_=x_view[a, :, il, :])
 
         load_x(0, True)
+        load_w(1, 0)
         load_x_tile(0, 0)
         load_w(0, 0)
         load_x_tile(0, 1)
-        load_w(1, 0)
         load_x_tile(0, 2)
         load_x_tile(0, 3)
         load_w(0, 1)

@@ -30,8 +30,7 @@ def tile_evidentialhead_pa_kernel(tc, x_bytes, x_scale, W1, b1, g, beta, out):
         keep = ctx.enter_context(tc.tile_pool(name="keep", bufs=1))
         stage = ctx.enter_context(tc.tile_pool(name="stage", bufs=2))
         small = ctx.enter_context(tc.tile_pool(name="small", bufs=4))
-        ps_hs = ctx.enter_context(tc.psum_pool(name="pshs", bufs=1))
-        ps_t = ctx.enter_context(tc.psum_pool(name="pst", bufs=7))
+        ps_t = ctx.enter_context(tc.psum_pool(name="pst", bufs=8))
 
         sc_b = keep.tile([P, D], F32, name="sc_b", tag="sc_b")
         nc.scalar.dma_start(out=sc_b[:], in_=x_scale.rearrange("o k -> (o k)").partition_broadcast(P))
@@ -153,13 +152,14 @@ def tile_evidentialhead_pa_kernel(tc, x_bytes, x_scale, W1, b1, g, beta, out):
         def epi1(i):
             a, il = divmod(i, GT)
             ts = slice(il * P, (il + 1) * P)
-            hs = ps_hs.tile([P, P], F32, name="hs", tag="hs")
+            hs_bank = ps_t.tile([P, 512], F32, name="tb", tag="tb")
+            hs = hs_bank[:, 0:P]
             for cb in range(NCB):
-                nc.tensor.matmul(out=hs[:], lhsT=hT[a][:, cb, ts], rhs=ident[:],
+                nc.tensor.matmul(out=hs, lhsT=hT[a][:, cb, ts], rhs=ident[:],
                                  start=(cb == 0), stop=(cb == NCB - 1), is_transpose=True)
             negmu = small.tile([P, 1], F32, name="negmu", tag="negmu")
             junk = stage.tile([P, 512], BF16, name="junk", tag="junk")
-            nc.scalar.activation(out=junk[:, 0:P], in_=hs[:], func=ACT.Identity, scale=-1.0 / H, accum_out=negmu[:])
+            nc.scalar.activation(out=junk[:, 0:P], in_=hs, func=ACT.Identity, scale=-1.0 / H, accum_out=negmu[:])
             hts = []
             for half in range(2):
                 ht = ps_t.tile([P, 512], F32, name="tb", tag="tb")

@@ -118,7 +118,7 @@ def tile_evidentialhead_pa_kernel(tc, x_bytes, x_scale, W1, b1, g, beta, out):
 
         def x_prep(i):
             a, il = divmod(i, GT)
-            xb = stage.tile([P, D], BF16, name="xb", tag="xb", bufs=3)
+            xb = stage.tile([P, D], BF16, name="xb", tag="xb", bufs=6)
             nc.vector.tensor_tensor(out=xb[:], in0=xby[a][:, il, :].bitcast(FP8), in1=sc_b[:], op=ALU.mult)
             words = xb[:].bitcast(F32)
             xt_bank = ps_t.tile([P, 512], F32, name="tb", tag="tb")
@@ -195,7 +195,7 @@ def tile_evidentialhead_pa_kernel(tc, x_bytes, x_scale, W1, b1, g, beta, out):
                                                op0=ALU.mult, op1=ALU.add)
                 nc.sync.dma_start(out=out[i * P:(i + 1) * P, cs], in_=o[:, cs])
 
-        xper = [1, 2, 2, 2, 1, 1, 1, 1, 1]
+        xper = [2] * ((NT - GT) // 2)
         LAG = 5
         w_interleave(1, 0, "v")
         x_prep(0)

@@ -34,12 +34,10 @@ def tile_evidentialhead_pa_kernel(tc, x_bytes, x_scale, W1, b1, g, beta, out):
 
         sc_b = keep.tile([P, D], F32, name="sc_b", tag="sc_b")
         nc.scalar.dma_start(out=sc_b[:], in_=x_scale.rearrange("o k -> (o k)").partition_broadcast(P))
-        b1c = keep.tile([P, NCB], BF16, name="b1c", tag="b1c")
-        with nc.allow_non_contiguous_dma(reason="bias: one element a partition, 1024 elements, once"):
-            nc.scalar.dma_start(out=b1c[:], in_=b1.rearrange("(c p) -> p c", p=P))
 
         w_view = W1.rearrange("(s p j) n -> s p j n", s=NPASS, j=4)
-        x_view = x_bytes.rearrange("(a i p) k -> a p i k", a=NG, i=GT)
+        x_view = x_bytes.rearrange("(a p i) k -> a p i k", a=NG, i=GT)
+        out_view = out.rearrange("(a p i) c -> a i p c", a=NG, i=GT)
         wraw = {}
         xby = {}
 
@@ -64,6 +62,9 @@ def tile_evidentialhead_pa_kernel(tc, x_bytes, x_scale, W1, b1, g, beta, out):
         load_x_tile(0, 1)
         load_x_tile(0, 2)
         load_x_tile(0, 3)
+        b1c = keep.tile([P, NCB], BF16, name="b1c", tag="b1c")
+        with nc.allow_non_contiguous_dma(reason="bias: one element a partition, 1024 elements, once"):
+            nc.sync.dma_start(out=b1c[:], in_=b1.rearrange("(c p) -> p c", p=P))
         load_w(0, 1)
         load_w(1, 1)
         load_x(1, False)
@@ -193,9 +194,9 @@ def tile_evidentialhead_pa_kernel(tc, x_bytes, x_scale, W1, b1, g, beta, out):
                 cs = slice(c * w, (c + 1) * w)
                 nc.vector.scalar_tensor_tensor(out=o[:, cs], in0=ys[i][:, cs], scalar=rstds[i][:], in1=beta_b[:, cs],
                                                op0=ALU.mult, op1=ALU.add)
-                nc.sync.dma_start(out=out[i * P:(i + 1) * P, cs], in_=o[:, cs])
+                nc.sync.dma_start(out=out_view[i // GT, i % GT][:, cs], in_=o[:, cs])
 
-        xper = [2] * ((NT - GT) // 2)
+        xper = [2, 2, 2, 2, 1, 1, 1, 1]
         LAG = 5
         w_interleave(1, 0, "v")
         x_prep(0)

@@ -62,9 +62,9 @@ def tile_evidentialhead_pa_kernel(tc, x_bytes, x_scale, W1, b1, g, beta, out):
         load_x_tile(0, 1)
         load_x_tile(0, 2)
         load_x_tile(0, 3)
-        b1c = keep.tile([P, NCB], BF16, name="b1c", tag="b1c")
-        with nc.allow_non_contiguous_dma(reason="bias: one element a partition, 1024 elements, once"):
-            nc.sync.dma_start(out=b1c[:], in_=b1.rearrange("(c p) -> p c", p=P))
+        b1r = keep.tile([P, P], BF16, name="b1r", tag="b1r")
+        nc.gpsimd.memset(b1r[:], 0.0)
+        nc.sync.dma_start(out=b1r[0:NCB, :], in_=b1.rearrange("(c p) -> c p", p=P))
         load_w(0, 1)
         load_w(1, 1)
         load_x(1, False)
@@ -83,8 +83,9 @@ def tile_evidentialhead_pa_kernel(tc, x_bytes, x_scale, W1, b1, g, beta, out):
         make_identity(nc, ident[:])
         neghalf = keep.tile([P, 1], F32, name="neghalf", tag="neghalf")
         nc.vector.memset(neghalf[:], -0.5)
+        identb = keep.tile([P, P], BF16, name="identb", tag="identb")
+        make_identity(nc, identb[:])
         b1f = keep.tile([P, NCB], F32, name="b1f", tag="b1f")
-        nc.gpsimd.tensor_copy(out=b1f[:], in_=b1c[:])
 
         wq = keep.tile([P, NPASS * H], U32, name="wq", tag="wq", align_bytes=64)
         ws = keep.tile([P, NPASS * H], U8, name="ws", tag="ws", align_bytes=64)
@@ -116,6 +117,11 @@ def tile_evidentialhead_pa_kernel(tc, x_bytes, x_scale, W1, b1, g, beta, out):
                 scales=ws[:, c0:c0 + 512],
                 in_=wgs[(s, nh)][:].rearrange("p n j -> p (n j)"),
             )
+
+        def bias_columns():
+            bank = ps_t.tile([P, 1024], BF16, name="tb", tag="tb")
+            nc.tensor.transpose(bank[:, 0:P], b1r[:], identb[:])
+            nc.scalar.copy(out=b1f[:], in_=bank[:, 0:NCB])
 
         def x_prep(i):
             a, il = divmod(i, GT)
@@ -206,6 +212,7 @@ def tile_evidentialhead_pa_kernel(tc, x_bytes, x_scale, W1, b1, g, beta, out):
         w_interleave(1, 1, "s")
         x_prep(2)
         x_prep(3)
+        bias_columns()
         w_quant(0, 0)
         x_quant(0)
 

@@ -33,7 +33,8 @@ def tile_evidentialhead_pa_kernel(tc, x_bytes, x_scale, W1, b1, g, beta, out):
         ps_t = ctx.enter_context(tc.psum_pool(name="pst", bufs=8))
 
         sc_b = keep.tile([P, D], F32, name="sc_b", tag="sc_b")
-        nc.scalar.dma_start(out=sc_b[:], in_=x_scale.rearrange("o k -> (o k)").partition_broadcast(P))
+        sc_c = keep.tile([P, D // P], F32, name="sc_c", tag="sc_c")
+        nc.scalar.dma_start(out=sc_c[:], in_=x_scale.rearrange("o (p j) -> (o p) j", p=P))
 
         w_view = W1.rearrange("(s p j) n -> s p j n", s=NPASS, j=4)
         x_view = x_bytes.rearrange("(a p i) k -> a p i k", a=NG, i=GT)
@@ -202,6 +203,20 @@ def tile_evidentialhead_pa_kernel(tc, x_bytes, x_scale, W1, b1, g, beta, out):
                                                op0=ALU.mult, op1=ALU.add)
                 nc.sync.dma_start(out=out_view[i // GT, i % GT][:, cs], in_=o[:, cs])
 
+        def spread_scales():
+            spread = sc_b[:].rearrange("q (p j) -> q p j", p=P)
+            for half in range(2):
+                bank = ps_t.tile([P, 512], F32, name="tb", tag="tb")
+                for j in range(4):
+                    nc.tensor.transpose(bank[:, j * P:(j + 1) * P],
+                                        sc_c[:, 4 * half + j:4 * half + j + 1].to_broadcast([P, P]), ident[:])
+                src = bank[:].rearrange("q (j p) -> q p j", j=4)
+                if half == 0:
+                    nc.vector.tensor_copy(out=spread[:, :, 0:4], in_=src)
+                else:
+                    nc.scalar.copy(out=spread[:, :, 4:8], in_=src)
+
+        spread_scales()
         xper = [2, 2, 2, 2, 1, 1, 1, 1]
         LAG = 5
         w_interleave(1, 0, "v")

@@ -34,7 +34,7 @@ def tile_evidentialhead_pa_kernel(tc, x_bytes, x_scale, W1, b1, g, beta, out):
 
         sc_b = keep.tile([P, D], F32, name="sc_b", tag="sc_b")
         sc_c = keep.tile([P, D // P], F32, name="sc_c", tag="sc_c")
-        nc.scalar.dma_start(out=sc_c[:], in_=x_scale.rearrange("o (p j) -> (o p) j", p=P))
+        nc.sync.dma_start(out=sc_c[:], in_=x_scale.rearrange("o (p j) -> (o p) j", p=P))
 
         w_view = W1.rearrange("(s p j) n -> s p j n", s=NPASS, j=4)
         x_view = x_bytes.rearrange("(a p i) k -> a p i k", a=NG, i=GT)
@@ -210,26 +210,24 @@ def tile_evidentialhead_pa_kernel(tc, x_bytes, x_scale, W1, b1, g, beta, out):
                 for j in range(4):
                     nc.tensor.transpose(bank[:, j * P:(j + 1) * P],
                                         sc_c[:, 4 * half + j:4 * half + j + 1].to_broadcast([P, P]), ident[:])
-                src = bank[:].rearrange("q (j p) -> q p j", j=4)
-                if half == 0:
-                    nc.vector.tensor_copy(out=spread[:, :, 0:4], in_=src)
-                else:
-                    nc.scalar.copy(out=spread[:, :, 4:8], in_=src)
+                nc.scalar.copy(out=spread[:, :, 4 * half:4 * half + 4], in_=bank[:].rearrange("q (j p) -> q p j", j=4))
 
-        spread_scales()
+        with tc.manual_schedule(engines={mybir.EngineType.Activation}):
+            spread_scales()
+            w_interleave(1, 0, "v")
+            w_interleave(0, 0, "s")
+            x_prep(0)
+            w_quant(1, 0)
+            x_prep(1)
+            x_prep(2)
+            x_prep(3)
+            bias_columns()
+            w_quant(0, 0)
+            x_quant(0)
+            w_interleave(1, 1, "s")
+            w_interleave(0, 1, "s")
         xper = [2, 2, 2, 2, 1, 1, 1, 1]
         LAG = 5
-        w_interleave(1, 0, "v")
-        x_prep(0)
-        w_interleave(0, 0, "s")
-        w_quant(1, 0)
-        x_prep(1)
-        w_interleave(1, 1, "s")
-        x_prep(2)
-        x_prep(3)
-        bias_columns()
-        w_quant(0, 0)
-        x_quant(0)
 
         nx = GT
         for t in range(NT + LAG + 1):
@@ -240,7 +238,6 @@ def tile_evidentialhead_pa_kernel(tc, x_bytes, x_scale, W1, b1, g, beta, out):
                 mm_silu(a, 2 * q)
                 mm_silu(a, 2 * q + 1)
                 if t == 0:
-                    w_interleave(0, 1, "s")
                     w_quant(1, 1)
                 if t == 1:
                     w_quant(0, 1)

from contextlib import ExitStack

import concourse.mybir as mybir
from concourse.masks import make_identity

B, D, H = 2048, 1024, 1024
FLOPS = 2 * B * D * H
EPS_LN = 1e-5

F32 = mybir.dt.float32
BF16 = mybir.dt.bfloat16
U32 = mybir.dt.uint32
U8 = mybir.dt.uint8
FP8 = mybir.dt.float8_e4m3fn
FP8X4 = mybir.dt.float8_e4m3fn_x4
ACT = mybir.ActivationFunctionType
ALU = mybir.AluOpType

P = 128
NT = B // P
GT = 4
NG = NT // GT
NCB = H // P
NPASS = D // 512


def tile_evidentialhead_pa_kernel(tc, x_bytes, x_scale, W1, b1, g, beta, out):
    nc = tc.nc
    with ExitStack() as ctx:
        keep = ctx.enter_context(tc.tile_pool(name="keep", bufs=1))
        stage = ctx.enter_context(tc.tile_pool(name="stage", bufs=2))
        small = ctx.enter_context(tc.tile_pool(name="small", bufs=4))
        ps_t = ctx.enter_context(tc.psum_pool(name="pst", bufs=8))

        sc_b = keep.tile([P, D], F32, name="sc_b", tag="sc_b")
        sc_c = keep.tile([P, D // P], F32, name="sc_c", tag="sc_c")
        nc.sync.dma_start(out=sc_c[:], in_=x_scale.rearrange("o (p j) -> (o p) j", p=P))

        w_view = W1.rearrange("(s p j) n -> s p j n", s=NPASS, j=4)
        x_view = x_bytes.rearrange("(a p i) k -> a p i k", a=NG, i=GT)
        out_view = out.rearrange("(a p i) c -> a i p c", a=NG, i=GT)
        wraw = {}
        xby = {}

        def load_w(s, nh):
            t = keep.tile([P, 4, 512], BF16, name="wraw%d%d" % (s, nh), tag="wraw%d%d" % (s, nh))
            nc.sync.dma_start(out=t[:], in_=w_view[s, :, :, nh * 512:(nh + 1) * 512])
            wraw[(s, nh)] = t

        def load_x(a, per_tile):
            t = keep.tile([P, GT, D], U8, name="xbytes%d" % a, tag="xbytes%d" % a)
            xby[a] = t
            if not per_tile:
                nc.sync.dma_start(out=t[:], in_=x_view[a])

        def load_x_tile(a, il):
            nc.sync.dma_start(out=xby[a][:, il, :], in_=x_view[a, :, il, :])

        load_x(0, True)
        load_w(1, 0)
        load_x_tile(0, 0)
        load_w(0, 0)
        load_x_tile(0, 1)
        load_x_tile(0, 2)
        load_x_tile(0, 3)
        b1r = keep.tile([P, P], BF16, name="b1r", tag="b1r")
        nc.gpsimd.memset(b1r[:], 0.0)
        nc.sync.dma_start(out=b1r[0:NCB, :], in_=b1.rearrange("(c p) -> c p", p=P))
        load_w(0, 1)
        load_w(1, 1)
        load_x(1, False)
        load_x(2, False)
        load_x(3, False)
        g_b = keep.tile([P, H], BF16, name="g_b", tag="g_b")
        nc.sync.dma_start(out=g_b[:], in_=g.partition_broadcast(P))
        beta_b = keep.tile([P, H], BF16, name="beta_b", tag="beta_b")
        nc.sync.dma_start(out=beta_b[:], in_=beta.partition_broadcast(P))

        warm = keep.tile([P, 1], F32, name="warm", tag="warm")
        nc.vector.memset(warm[:], 0.0)
        warm2 = keep.tile([P, 1], F32, name="warm2", tag="warm2")
        nc.scalar.activation(out=warm2[:], in_=warm[:], func=ACT.Silu)
        ident = keep.tile([P, P], F32, name="ident", tag="ident")
        make_identity(nc, ident[:])
        neghalf = keep.tile([P, 1], F32, name="neghalf", tag="neghalf")
        nc.vector.memset(neghalf[:], -0.5)
        identb = keep.tile([P, P], BF16, name="identb", tag="identb")
        make_identity(nc, identb[:])
        b1f = keep.tile([P, NCB], F32, name="b1f", tag="b1f")

        wq = keep.tile([P, NPASS * H], U32, name="wq", tag="wq", align_bytes=64)
        ws = keep.tile([P, NPASS * H], U8, name="ws", tag="ws", align_bytes=64)
        xg = {}
        xq = {}
        xs = {}
        for a in range(NG):
            xg[a] = keep.tile([P, NPASS * 512 * 4], BF16, name="xg%d" % a, tag="xg%d" % a, align_bytes=64)
            xq[a] = keep.tile([P, NPASS * 512], U32, name="xq%d" % a, tag="xq%d" % a, align_bytes=64)
            xs[a] = keep.tile([P, NPASS * 512], U8, name="xs%d" % a, tag="xs%d" % a, align_bytes=64)
        wgs = {}
        hT = {}
        ys = {}
        rstds = {}

        def w_interleave(s, nh, eng):
            wg = stage.tile([P, 512, 4], BF16, name="wg", tag="wg", align_bytes=64)
            src = wraw[(s, nh)][:].rearrange("p j n -> p n j")
            if eng == "v":
                nc.vector.tensor_copy(out=wg[:], in_=src)
            else:
                nc.scalar.copy(out=wg[:], in_=src)
            wgs[(s, nh)] = wg

        def w_quant(s, nh):
            c0 = s * H + nh * 512
            nc.vector.quantize_mx(
                out=wq[:, c0:c0 + 512].bitcast(FP8X4),
                scales=ws[:, c0:c0 + 512],
                in_=wgs[(s, nh)][:].rearrange("p n j -> p (n j)"),
            )

        def bias_columns():
            bank = ps_t.tile([P, 1024], BF16, name="tb", tag="tb")
            nc.tensor.transpose(bank[:, 0:P], b1r[:], identb[:])
            nc.scalar.copy(out=b1f[:], in_=bank[:, 0:NCB])

        def x_prep(i):
            a, il = divmod(i, GT)
            xb = stage.tile([P, D], BF16, name="xb", tag="xb", bufs=6)
            nc.vector.tensor_tensor(out=xb[:], in0=xby[a][:, il, :].bitcast(FP8), in1=sc_b[:], op=ALU.mult)
            words = xb[:].bitcast(F32)
            xt_bank = ps_t.tile([P, 512], F32, name="tb", tag="tb")
            xt = xt_bank[:].rearrange("p (s u r) -> p s u r", s=NPASS, u=2)
            for s in range(NPASS):
                for u in range(2):
                    nc.tensor.transpose(xt[:, s, u, :], words[:, 256 * s + u:256 * (s + 1):2], ident[:])
            xgw = xg[a][:].bitcast(F32).rearrange("p (s r u) -> p s r u", s=NPASS, u=2)
            nc.scalar.copy(out=xgw[:, :, il * P:(il + 1) * P, :], in_=xt.rearrange("p s u r -> p s r u"))

        def x_quant(a):
            nc.vector.quantize_mx(out=xq[a][:].bitcast(FP8X4), scales=xs[a][:], in_=xg[a][:])

        def mm_silu(a, cb):
            if cb == 0:
                hT[a] = stage.tile([P, NCB, 512], F32, name="hT", tag="hT", bufs=3)
            mm = ps_t.tile([P, 512], F32, name="tb", tag="tb")
            for s in range(NPASS):
                c0 = s * H + cb * P
                nc.tensor.matmul_mx(
                    out=mm[:],
                    lhsT=wq[:, c0:c0 + P].bitcast(FP8X4),
                    lhsT_scale=ws[:, c0:c0 + P],
                    rhs=xq[a][:, s * 512:(s + 1) * 512].bitcast(FP8X4),
                    rhs_scale=xs[a][:, s * 512:(s + 1) * 512],
                    start=(s == 0),
                    stop=(s == NPASS - 1),
                )
            nc.scalar.activation(out=hT[a][:, cb, :], in_=mm[:], func=ACT.Silu, bias=b1f[:, cb:cb + 1])

        def epi1(i):
            a, il = divmod(i, GT)
            ts = slice(il * P, (il + 1) * P)
            hs_bank = ps_t.tile([P, 512], F32, name="tb", tag="tb")
            hs = hs_bank[:, 0:P]
            for cb in range(NCB):
                nc.tensor.matmul(out=hs, lhsT=hT[a][:, cb, ts], rhs=ident[:],
                                 start=(cb == 0), stop=(cb == NCB - 1), is_transpose=True)
            negmu = small.tile([P, 1], F32, name="negmu", tag="negmu")
            junk = stage.tile([P, 512], BF16, name="junk", tag="junk")
            nc.scalar.activation(out=junk[:, 0:P], in_=hs, func=ACT.Identity, scale=-1.0 / H, accum_out=negmu[:])
            hts = []
            for half in range(2):
                ht = ps_t.tile([P, 512], F32, name="tb", tag="tb")
                for j in range(4):
                    nc.tensor.transpose(ht[:, j * P:(j + 1) * P], hT[a][:, 4 * half + j, ts], ident[:])
                hts.append(ht)
            ssq = small.tile([P, 2], F32, name="ssq", tag="ssq")
            for half in range(2):
                junk2 = stage.tile([P, 512], BF16, name="junk", tag="junk")
                nc.scalar.activation(out=junk2[:], in_=hts[half][:], func=ACT.Square, bias=negmu[:],
                                     accum_out=ssq[:, half:half + 1])
            y = stage.tile([P, H], F32, name="y", tag="y", bufs=4)
            for half in range(2):
                cs = slice(half * 512, (half + 1) * 512)
                nc.vector.scalar_tensor_tensor(out=y[:, cs], in0=hts[half][:], scalar=negmu[:], in1=g_b[:, cs],
                                               op0=ALU.add, op1=ALU.mult)
            ve = small.tile([P, 1], F32, name="ve", tag="ve")
            junk3 = small.tile([P, 2], F32, name="junk3", tag="junk3")
            nc.scalar.activation(out=junk3[:], in_=ssq[:], func=ACT.Copy, scale=1.0 / H, bias=EPS_LN / 2.0,
                                 accum_out=ve[:])
            rstd = small.tile([P, 1], F32, name="rstd", tag="rstd")
            nc.gpsimd.tensor_tensor(out=rstd[:], in0=ve[:], in1=neghalf[:], op=ALU.pow)
            ys[i] = y
            rstds[i] = rstd

        def epi2(i):
            o = stage.tile([P, H], F32, name="o", tag="o", bufs=3)
            pieces = 2 if i == NT - 1 else 1
            w = H // pieces
            for c in range(pieces):
                cs = slice(c * w, (c + 1) * w)
                nc.vector.scalar_tensor_tensor(out=o[:, cs], in0=ys[i][:, cs], scalar=rstds[i][:], in1=beta_b[:, cs],
                                               op0=ALU.mult, op1=ALU.add)
                nc.sync.dma_start(out=out_view[i // GT, i % GT][:, cs], in_=o[:, cs])

        def spread_scales():
            spread = sc_b[:].rearrange("q (p j) -> q p j", p=P)
            for half in range(2):
                bank = ps_t.tile([P, 512], F32, name="tb", tag="tb")
                for j in range(4):
                    nc.tensor.transpose(bank[:, j * P:(j + 1) * P],
                                        sc_c[:, 4 * half + j:4 * half + j + 1].to_broadcast([P, P]), ident[:])
                nc.scalar.copy(out=spread[:, :, 4 * half:4 * half + 4], in_=bank[:].rearrange("q (j p) -> q p j", j=4))

        with tc.manual_schedule(engines={mybir.EngineType.Activation}):
            spread_scales()
            w_interleave(1, 0, "v")
            w_interleave(0, 0, "s")
            x_prep(0)
            w_quant(1, 0)
            x_prep(1)
            x_prep(2)
            x_prep(3)
            bias_columns()
            w_quant(0, 0)
            x_quant(0)
            w_interleave(1, 1, "s")
            w_interleave(0, 1, "s")
        xper = [2, 2, 2, 2, 1, 1, 1, 1]
        LAG = 5

        nx = GT
        for t in range(NT + LAG + 1):
            if LAG <= t < NT + LAG:
                epi1(t - LAG)
            if t < NT:
                a, q = divmod(t, GT)
                mm_silu(a, 2 * q)
                mm_silu(a, 2 * q + 1)
                if t == 0:
                    w_quant(1, 1)
                if t == 1:
                    w_quant(0, 1)
            for rep in range(xper[t] if t < len(xper) else 0):
                if nx < NT:
                    x_prep(nx)
                    if nx % GT == GT - 1:
                        x_quant(nx // GT)
                    nx += 1
            if t >= LAG + 1:
                epi2(t - LAG - 1)
